import numpy as np
import ml_dtypes


def mxq(x, axis, fmt="e4m3"):
    dtype, down = {"e4m3": (ml_dtypes.float8_e4m3fn, 7), "e5m2": (ml_dtypes.float8_e5m2, 14)}[fmt]
    v = np.moveaxis(np.asarray(x, np.float32).astype(ml_dtypes.bfloat16).astype(np.float64), axis, -1)
    blocks = v.reshape(v.shape[:-1] + (-1, 32))
    amax = np.abs(blocks).max(-1, keepdims=True)
    byte = np.maximum(np.where(amax > 0, np.frexp(amax)[1] - 1 + 127, 0) - down, 1)
    scale = np.exp2(byte - 127.0)
    codes = (blocks / scale).astype(np.float32).astype(dtype).astype(np.float64)
    return np.moveaxis((codes * scale).reshape(v.shape), -1, axis)


WIDE = False


def mx_kscale(k):
    if not WIDE:
        return np.ones(k)
    levels = np.array([10, -10, 5, -5, 0])
    a = np.random.permutation(np.resize(levels, k // 512 * 4)).reshape(k // 512, 4)
    idx = np.arange(k)
    return np.exp2(a[idx // 512, idx % 128 // 32])


BF16 = ml_dtypes.bfloat16


def bf(x):
    return np.asarray(x, np.float32).astype(BF16)


def f64(x):
    return np.asarray(x).astype(np.float64)


B, L, D, DK = 4, 512, 1024, 128


def setup_inputs():
    s = mx_kscale(D)
    z = np.random.standard_normal((B, L, L)) * 2.0
    e = np.exp(z - z.max(-1, keepdims=True))
    return {"x": bf(np.random.standard_normal((B, L, D)) * s),
            "Wv1": bf(np.random.standard_normal((D, D)) * 2.0 / np.sqrt(D) / s),
            "bv1": bf(np.random.standard_normal(D) * 0.5),
            "att2": bf(e / e.sum(-1, keepdims=True)),
            "gamma2": bf(1.0 + 0.1 * np.random.standard_normal(1)),
            "y": bf(np.random.standard_normal((B, L, D)))}


def reference(x, Wv1, bv1, att2, gamma2, y):
    v1 = (mxq(f64(x), 2, "e4m3") @ mxq(f64(Wv1).T, 0, "e4m3")) + f64(bv1)
    o = mxq(v1.transpose(0, 2, 1), 2, "e4m3") @ mxq(f64(att2), 1, "e4m3")
    return f64(gamma2) * o.reshape(B, L, D) + f64(y)

@@ -1,0 +1,209 @@
+from contextlib import ExitStack
+
+import concourse.mybir as mybir
+from concourse.masks import make_identity
+
+F32 = mybir.dt.float32
+BF16 = mybir.dt.bfloat16
+U32 = mybir.dt.uint32
+U8 = mybir.dt.uint8
+FP8X4 = mybir.dt.float8_e4m3fn_x4
+ADD = mybir.AluOpType.add
+MULT = mybir.AluOpType.mult
+
+P = 128
+PACK = 4
+K_PASS = P * PACK
+B = 4
+L = 512
+D = 1024
+BANK = 512
+PASSES = D // K_PASS
+D_TILES = D // P
+GROUP = 4
+STORE_TILES = 2
+
+FLOPS = 2 * B * L * D * D + 2 * B * D * L * L
+
+
+def operand_cols(tile_index, k_pass):
+    first = (tile_index * PASSES + k_pass) * P
+    return slice(first, first + P)
+
+
+def transpose_rows(nc, psum_t, ident, rows, grouped):
+    words = rows.bitcast(F32)
+    grouped_words = grouped.bitcast(F32)
+    for i in range(GROUP):
+        bank = psum_t.tile([P, BANK], F32)
+        for c in range(BANK // P):
+            nc.tensor.transpose(
+                bank[:, c * P : (c + 1) * P],
+                words[:, i * BANK + c * P : i * BANK + (c + 1) * P],
+                ident,
+            )
+        nc.scalar.copy(
+            out=grouped_words[:, i * BANK : (i + 1) * BANK].rearrange(
+                "p (g r u) -> p g r u", g=PASSES, u=2
+            ),
+            in_=bank[:].rearrange("p (g u r) -> p g r u", g=PASSES, u=2),
+        )
+
+
+def tile_dualcrossmodalattention_pb_kernel(tc, x, Wv1, bv1, att2, gamma2, y, out):
+    nc = tc.nc
+    with ExitStack() as ctx:
+        const = ctx.enter_context(tc.tile_pool(name="const", bufs=1))
+        loads = ctx.enter_context(tc.tile_pool(name="loads", bufs=B))
+        stage = ctx.enter_context(tc.tile_pool(name="stage", bufs=2))
+        psum_t = ctx.enter_context(tc.psum_pool(name="psum_t", bufs=2))
+        psum_v = ctx.enter_context(tc.psum_pool(name="psum_v", bufs=3))
+        psum_o = ctx.enter_context(tc.psum_pool(name="psum_o", bufs=3))
+
+        ident = const.tile([P, P], F32)
+        make_identity(nc, ident[:])
+
+        def load(pool, tag, width, rows_view):
+            landed = pool.tile([P, width], BF16, tag=tag)
+            nc.sync.dma_start(out=landed[:], in_=rows_view)
+            return landed
+
+        def load_x(b):
+            return load(loads, "x", PACK * D, x[b].rearrange("(p t) k -> p (t k)", t=PACK))
+
+        x_sb = [load_x(0)]
+        w_sb = const.tile([P, D_TILES * D], BF16)
+        w_view = Wv1.rearrange("(p j) k -> p (j k)", j=D_TILES)
+        for h in range(D_TILES // GROUP):
+            cols = slice(h * GROUP * D, (h + 1) * GROUP * D)
+            nc.sync.dma_start(out=w_sb[:, cols], in_=w_view[:, cols])
+        bias_bc = const.tile([P, D], BF16)
+        nc.sync.dma_start(out=bias_bc[:], in_=bv1.partition_broadcast(P))
+        gamma_bf = const.tile([P, 1], BF16)
+        nc.sync.dma_start(out=gamma_bf[:], in_=gamma2.partition_broadcast(P))
+        att_sb = []
+        y_sb = []
+        for b in range(B):
+            att_sb.append(
+                load(loads, "att", PACK * L, att2[b].rearrange("(p t) m -> p (t m)", t=PACK))
+            )
+            if b + 1 < B:
+                x_sb.append(load_x(b + 1))
+            y_sb.append(
+                load(loads, "y", D_TILES * L, y[b].rearrange("(p a) c -> p (a c)", a=PACK))
+            )
+
+        def transposed(rows):
+            grouped = stage.tile([P, GROUP * D], BF16, tag="grouped", align_bytes=64)
+            transpose_rows(nc, psum_t, ident[:], rows, grouped[:])
+            return grouped
+
+        def quantise(grouped, pool, tag):
+            words = grouped.shape[1] // PACK
+            codes = pool.tile([P, words], U32, tag=tag + "_codes", align_bytes=64)
+            scales = pool.tile([P, words], U8, tag=tag + "_scales", align_bytes=64)
+            nc.vector.quantize_mx(out=codes[:].bitcast(FP8X4), scales=scales[:], in_=grouped[:])
+            return codes, scales
+
+        def regroup_att(b):
+            att_grouped = stage.tile([P, PACK * L], BF16, tag="att_grouped", align_bytes=64)
+            nc.scalar.copy(
+                out=att_grouped[:].rearrange("p (c i t) -> p c t i", i=4, t=PACK),
+                in_=att_sb[b][:].rearrange("p (t c i) -> p c t i", t=PACK, i=4),
+            )
+            return att_grouped
+
+        def first_matmul(x_q, j, v_grouped):
+            x_codes, x_scales = x_q
+            w_codes, w_scales = w_q[j // GROUP]
+            v_ps = psum_v.tile([P, BANK], F32)
+            for t in range(PACK):
+                for g in range(PASSES):
+                    nc.tensor.matmul_mx(
+                        out=v_ps[:, t * P : (t + 1) * P],
+                        lhsT=x_codes[:, operand_cols(t, g)].bitcast(FP8X4),
+                        lhsT_scale=x_scales[:, operand_cols(t, g)],
+                        rhs=w_codes[:, operand_cols(j % GROUP, g)].bitcast(FP8X4),
+                        rhs_scale=w_scales[:, operand_cols(j % GROUP, g)],
+                        start=(g == 0),
+                        stop=(g == PASSES - 1),
+                    )
+            nc.vector.tensor_tensor(
+                out=v_grouped[:, j * BANK : (j + 1) * BANK].rearrange("p (r t) -> p r t", t=PACK),
+                in0=v_ps[:].rearrange("p (t r) -> p r t", t=PACK),
+                in1=bias_by_tile[:, j, :].unsqueeze(2).to_broadcast([P, P, PACK]),
+                op=ADD,
+            )
+
+        def second_matmul(b, v_q, att_q, j, out_sb):
+            v_codes, v_scales = v_q
+            att_codes, att_scales = att_q
+            o_ps = psum_o.tile([P, BANK], F32)
+            nc.tensor.matmul_mx(
+                out=o_ps[:],
+                lhsT=v_codes[:, j * P : (j + 1) * P].bitcast(FP8X4),
+                lhsT_scale=v_scales[:, j * P : (j + 1) * P],
+                rhs=att_codes[:].bitcast(FP8X4),
+                rhs_scale=att_scales[:],
+                start=True,
+                stop=True,
+            )
+            cols = slice(j * L, (j + 1) * L)
+            nc.vector.scalar_tensor_tensor(
+                out=out_sb[:, cols],
+                in0=o_ps[:],
+                scalar=gamma[:, 0:1],
+                in1=y_sb[b][:, cols],
+                op0=MULT,
+                op1=ADD,
+            )
+
+        x_next = quantise(transposed(x_sb[0][:]), stage, "x")
+        w_q = []
+        for h in range(D_TILES // GROUP):
+            w_grouped = transposed(w_sb[:, h * GROUP * D : (h + 1) * GROUP * D])
+            w_q.append(quantise(w_grouped, const, "w%d" % h))
+
+        bias_by_tile = const.tile([P, D_TILES, P], F32)
+        nc.vector.tensor_copy(
+            out=bias_by_tile[:], in_=bias_bc[:].rearrange("p (r j) -> p j r", j=D_TILES)
+        )
+        gamma = const.tile([P, 1], F32)
+        nc.vector.tensor_copy(out=gamma[:], in_=gamma_bf[:])
+
+        v_q = None
+        att_q = None
+        for s in range(B + 1):
+            x_q = x_next
+            v_prev = v_q
+            att_prev = att_q
+            if s + 1 < B:
+                x_grouped = transposed(x_sb[s + 1][:])
+            if s < B:
+                att_grouped = regroup_att(s)
+                v_grouped = stage.tile([P, D_TILES * BANK], BF16, tag="v_grouped", align_bytes=64)
+                v_codes = stage.tile([P, D], U32, tag="v_codes", align_bytes=64)
+                v_scales = stage.tile([P, D], U8, tag="v_scales", align_bytes=64)
+                v_q = (v_codes, v_scales)
+            if s > 0:
+                out_sb = stage.tile([P, D_TILES * L], F32, tag="out_sb")
+                out_view = out[s - 1].rearrange("(p a) c -> p (a c)", a=PACK)
+            for h in range(D_TILES // GROUP):
+                for j in range(h * GROUP, (h + 1) * GROUP):
+                    if s < B:
+                        first_matmul(x_q, j, v_grouped)
+                    if s > 0:
+                        second_matmul(s - 1, v_prev, att_prev, j, out_sb)
+                        if (j + 1) % STORE_TILES == 0:
+                            cols = slice((j + 1 - STORE_TILES) * L, (j + 1) * L)
+                            nc.sync.dma_start(out=out_view[:, cols], in_=out_sb[:, cols])
+                if s < B:
+                    nc.vector.quantize_mx(
+                        out=v_codes[:, h * GROUP * P : (h + 1) * GROUP * P].bitcast(FP8X4),
+                        scales=v_scales[:, h * GROUP * P : (h + 1) * GROUP * P],
+                        in_=v_grouped[:, h * GROUP * BANK : (h + 1) * GROUP * BANK],
+                    )
+                if h == 0 and s + 1 < B:
+                    x_next = quantise(x_grouped, stage, "x")
+                if h == 1 and s < B:
+                    att_q = quantise(att_grouped, stage, "att")

@@ -10,6 +10,7 @@ U8 = mybir.dt.uint8
 FP8X4 = mybir.dt.float8_e4m3fn_x4
 ADD = mybir.AluOpType.add
 MULT = mybir.AluOpType.mult
+COPY = mybir.ActivationFunctionType.Copy
 
 P = 128
 PACK = 4
@@ -19,112 +20,92 @@ L = 512
 D = 1024
 BANK = 512
 PASSES = D // K_PASS
+TILE_WORDS = D // PACK
 D_TILES = D // P
-GROUP = 4
-STORE_TILES = 2
+RUN = 2
+RUNS = D_TILES // RUN
+PREPARE_IN_RUN = 2
 
 FLOPS = 2 * B * L * D * D + 2 * B * D * L * L
-
-
-def operand_cols(tile_index, k_pass):
-    first = (tile_index * PASSES + k_pass) * P
-    return slice(first, first + P)
-
-
-def transpose_rows(nc, psum_t, ident, rows, grouped):
-    words = rows.bitcast(F32)
-    grouped_words = grouped.bitcast(F32)
-    for i in range(GROUP):
-        bank = psum_t.tile([P, BANK], F32)
-        for c in range(BANK // P):
-            nc.tensor.transpose(
-                bank[:, c * P : (c + 1) * P],
-                words[:, i * BANK + c * P : i * BANK + (c + 1) * P],
-                ident,
-            )
-        nc.scalar.copy(
-            out=grouped_words[:, i * BANK : (i + 1) * BANK].rearrange(
-                "p (g r u) -> p g r u", g=PASSES, u=2
-            ),
-            in_=bank[:].rearrange("p (g u r) -> p g r u", g=PASSES, u=2),
-        )
 
 
 def tile_dualcrossmodalattention_pb_kernel(tc, x, Wv1, bv1, att2, gamma2, y, out):
     nc = tc.nc
     with ExitStack() as ctx:
+        ctx.enter_context(tc.manual_schedule())
         const = ctx.enter_context(tc.tile_pool(name="const", bufs=1))
         loads = ctx.enter_context(tc.tile_pool(name="loads", bufs=B))
         stage = ctx.enter_context(tc.tile_pool(name="stage", bufs=2))
-        psum_t = ctx.enter_context(tc.psum_pool(name="psum_t", bufs=2))
         psum_v = ctx.enter_context(tc.psum_pool(name="psum_v", bufs=3))
-        psum_o = ctx.enter_context(tc.psum_pool(name="psum_o", bufs=3))
+        psum_s = ctx.enter_context(tc.psum_pool(name="psum_s", bufs=5))
 
         ident = const.tile([P, P], F32)
         make_identity(nc, ident[:])
+        ones = const.tile([P, P], BF16)
+        nc.vector.memset(ones[:], 1.0)
+        bias_row = const.tile([P, D], BF16)
+        nc.vector.memset(bias_row[:], 0.0)
 
-        def load(pool, tag, width, rows_view):
+        def load(pool, tag, rows_view, pieces):
+            width = rows_view.shape[1]
             landed = pool.tile([P, width], BF16, tag=tag)
-            nc.sync.dma_start(out=landed[:], in_=rows_view)
+            for piece in range(pieces):
+                cols = slice(piece * width // pieces, (piece + 1) * width // pieces)
+                nc.sync.dma_start(out=landed[:, cols], in_=rows_view[:, cols])
             return landed
 
-        def load_x(b):
-            return load(loads, "x", PACK * D, x[b].rearrange("(p t) k -> p (t k)", t=PACK))
+        def load_x(b, pieces):
+            return load(loads, "x", x[b].rearrange("(p t) k -> p (t k)", t=PACK), pieces)
 
-        x_sb = [load_x(0)]
-        w_sb = const.tile([P, D_TILES * D], BF16)
-        w_view = Wv1.rearrange("(p j) k -> p (j k)", j=D_TILES)
-        for h in range(D_TILES // GROUP):
-            cols = slice(h * GROUP * D, (h + 1) * GROUP * D)
-            nc.sync.dma_start(out=w_sb[:, cols], in_=w_view[:, cols])
-        bias_bc = const.tile([P, D], BF16)
-        nc.sync.dma_start(out=bias_bc[:], in_=bv1.partition_broadcast(P))
+        x_sb = [load_x(0, PACK)]
+        nc.sync.dma_start(out=bias_row[0:1, :], in_=bv1.unsqueeze(0))
         gamma_bf = const.tile([P, 1], BF16)
         nc.sync.dma_start(out=gamma_bf[:], in_=gamma2.partition_broadcast(P))
+        w_sb = load(const, "w", Wv1.rearrange("(p j) k -> p (j k)", j=D_TILES), RUNS)
         att_sb = []
         y_sb = []
         for b in range(B):
-            att_sb.append(
-                load(loads, "att", PACK * L, att2[b].rearrange("(p t) m -> p (t m)", t=PACK))
-            )
             if b + 1 < B:
-                x_sb.append(load_x(b + 1))
-            y_sb.append(
-                load(loads, "y", D_TILES * L, y[b].rearrange("(p a) c -> p (a c)", a=PACK))
+                x_sb.append(load_x(b + 1, 1))
+            att_sb.append(load(loads, "att", att2[b].rearrange("(p t) m -> p (t m)", t=PACK), 1))
+            y_sb.append(load(loads, "y", y[b].rearrange("(p a) c -> p (a c)", a=PACK), 1))
+
+        def transpose_tile(rows, grouped):
+            bank = psum_s.tile([P, BANK], F32, tag="bank")
+            words = rows.bitcast(F32)
+            for chunk in range(BANK // P):
+                cols = slice(chunk * P, (chunk + 1) * P)
+                nc.tensor.transpose(bank[:, cols], words[:, cols], ident[:])
+            nc.scalar.copy(
+                out=grouped.bitcast(F32).rearrange("p (g r u) -> p g r u", g=PASSES, u=2),
+                in_=bank[:].rearrange("p (g u r) -> p g r u", g=PASSES, u=2),
             )
 
-        def transposed(rows):
-            grouped = stage.tile([P, GROUP * D], BF16, tag="grouped", align_bytes=64)
-            transpose_rows(nc, psum_t, ident[:], rows, grouped[:])
-            return grouped
-
-        def quantise(grouped, pool, tag):
-            words = grouped.shape[1] // PACK
+        def mx_tiles(pool, tag, words):
             codes = pool.tile([P, words], U32, tag=tag + "_codes", align_bytes=64)
             scales = pool.tile([P, words], U8, tag=tag + "_scales", align_bytes=64)
-            nc.vector.quantize_mx(out=codes[:].bitcast(FP8X4), scales=scales[:], in_=grouped[:])
             return codes, scales
 
-        def regroup_att(b):
-            att_grouped = stage.tile([P, PACK * L], BF16, tag="att_grouped", align_bytes=64)
-            nc.scalar.copy(
-                out=att_grouped[:].rearrange("p (c i t) -> p c t i", i=4, t=PACK),
-                in_=att_sb[b][:].rearrange("p (t c i) -> p c t i", t=PACK, i=4),
-            )
-            return att_grouped
+        def operand(mx, first, words):
+            codes, scales = mx
+            return codes[:, first : first + words].bitcast(FP8X4), scales[:, first : first + words]
+
+        def quantise(grouped, mx, first):
+            codes, scales = operand(mx, first, grouped.shape[1] // PACK)
+            nc.vector.quantize_mx(out=codes, scales=scales, in_=grouped)
 
         def first_matmul(x_q, j, v_grouped):
-            x_codes, x_scales = x_q
-            w_codes, w_scales = w_q[j // GROUP]
             v_ps = psum_v.tile([P, BANK], F32)
             for t in range(PACK):
                 for g in range(PASSES):
+                    x_codes, x_scales = operand(x_q, t * TILE_WORDS + g * P, P)
+                    w_codes, w_scales = operand(w_q, j * TILE_WORDS + g * P, P)
                     nc.tensor.matmul_mx(
                         out=v_ps[:, t * P : (t + 1) * P],
-                        lhsT=x_codes[:, operand_cols(t, g)].bitcast(FP8X4),
-                        lhsT_scale=x_scales[:, operand_cols(t, g)],
-                        rhs=w_codes[:, operand_cols(j % GROUP, g)].bitcast(FP8X4),
-                        rhs_scale=w_scales[:, operand_cols(j % GROUP, g)],
+                        lhsT=x_codes,
+                        lhsT_scale=x_scales,
+                        rhs=w_codes,
+                        rhs_scale=w_scales,
                         start=(g == 0),
                         stop=(g == PASSES - 1),
                     )
@@ -136,40 +117,73 @@ def tile_dualcrossmodalattention_pb_kernel(tc, x, Wv1, bv1, att2, gamma2, y, out
             )
 
         def second_matmul(b, v_q, att_q, j, out_sb):
-            v_codes, v_scales = v_q
-            att_codes, att_scales = att_q
-            o_ps = psum_o.tile([P, BANK], F32)
+            v_codes, v_scales = operand(v_q, j * P, P)
+            att_codes, att_scales = operand(att_q, 0, L)
+            o_ps = psum_s.tile([P, BANK], F32, tag="bank")
             nc.tensor.matmul_mx(
                 out=o_ps[:],
-                lhsT=v_codes[:, j * P : (j + 1) * P].bitcast(FP8X4),
-                lhsT_scale=v_scales[:, j * P : (j + 1) * P],
-                rhs=att_codes[:].bitcast(FP8X4),
-                rhs_scale=att_scales[:],
+                lhsT=v_codes,
+                lhsT_scale=v_scales,
+                rhs=att_codes,
+                rhs_scale=att_scales,
                 start=True,
                 stop=True,
             )
             cols = slice(j * L, (j + 1) * L)
-            nc.vector.scalar_tensor_tensor(
-                out=out_sb[:, cols],
-                in0=o_ps[:],
-                scalar=gamma[:, 0:1],
-                in1=y_sb[b][:, cols],
-                op0=MULT,
-                op1=ADD,
-            )
+            if j % RUN == 0:
+                nc.scalar.activation(out=out_sb[:, cols], in_=o_ps[:], func=COPY, scale=gamma[:, 0:1])
+                nc.gpsimd.tensor_tensor(
+                    out=out_sb[:, cols], in0=out_sb[:, cols], in1=y_sb[b][:, cols], op=ADD
+                )
+            else:
+                nc.vector.scalar_tensor_tensor(
+                    out=out_sb[:, cols],
+                    in0=o_ps[:],
+                    scalar=gamma[:, 0:1],
+                    in1=y_sb[b][:, cols],
+                    op0=MULT,
+                    op1=ADD,
+                )
 
-        x_next = quantise(transposed(x_sb[0][:]), stage, "x")
-        w_q = []
-        for h in range(D_TILES // GROUP):
-            w_grouped = transposed(w_sb[:, h * GROUP * D : (h + 1) * GROUP * D])
-            w_q.append(quantise(w_grouped, const, "w%d" % h))
+        def transpose_x(b):
+            x_grouped = stage.tile([P, PACK * D], BF16, tag="x_grouped", align_bytes=64)
+            for t in range(PACK):
+                cols = slice(t * D, (t + 1) * D)
+                transpose_tile(x_sb[b][:, cols], x_grouped[:, cols])
+            return x_grouped
+
+        def transpose_w(run):
+            w_grouped = stage.tile([P, RUN * D], BF16, tag="w_grouped", align_bytes=64)
+            for i in range(RUN):
+                j = run * RUN + i
+                transpose_tile(w_sb[:, j * D : (j + 1) * D], w_grouped[:, i * D : (i + 1) * D])
+            return w_grouped
+
+        x_grouped = transpose_x(0)
+        x_next = mx_tiles(stage, "x", PACK * TILE_WORDS)
+        for t in range(PACK):
+            quantise(x_grouped[:, t * D : (t + 1) * D], x_next, t * TILE_WORDS)
 
         bias_by_tile = const.tile([P, D_TILES, P], F32)
-        nc.vector.tensor_copy(
-            out=bias_by_tile[:], in_=bias_bc[:].rearrange("p (r j) -> p j r", j=D_TILES)
-        )
+        for half in range(D // BANK):
+            bias_ps = psum_s.tile([P, BANK], F32, tag="bank")
+            nc.tensor.matmul(
+                bias_ps[:],
+                lhsT=ones[:],
+                rhs=bias_row[:, half * BANK : (half + 1) * BANK],
+                start=True,
+                stop=True,
+            )
+            rows = BANK // D_TILES
+            nc.vector.tensor_copy(
+                out=bias_by_tile[:, :, half * rows : (half + 1) * rows],
+                in_=bias_ps[:].rearrange("p (r j) -> p j r", j=D_TILES),
+            )
         gamma = const.tile([P, 1], F32)
         nc.vector.tensor_copy(out=gamma[:], in_=gamma_bf[:])
+
+        w_q = mx_tiles(const, "w", D_TILES * TILE_WORDS)
+        quantise(transpose_w(0)[:], w_q, 0)
 
         v_q = None
         att_q = None
@@ -177,33 +191,41 @@ def tile_dualcrossmodalattention_pb_kernel(tc, x, Wv1, bv1, att2, gamma2, y, out
             x_q = x_next
             v_prev = v_q
             att_prev = att_q
-            if s + 1 < B:
-                x_grouped = transposed(x_sb[s + 1][:])
             if s < B:
-                att_grouped = regroup_att(s)
                 v_grouped = stage.tile([P, D_TILES * BANK], BF16, tag="v_grouped", align_bytes=64)
-                v_codes = stage.tile([P, D], U32, tag="v_codes", align_bytes=64)
-                v_scales = stage.tile([P, D], U8, tag="v_scales", align_bytes=64)
-                v_q = (v_codes, v_scales)
+                v_q = mx_tiles(stage, "v", D_TILES * P)
             if s > 0:
                 out_sb = stage.tile([P, D_TILES * L], F32, tag="out_sb")
                 out_view = out[s - 1].rearrange("(p a) c -> p (a c)", a=PACK)
-            for h in range(D_TILES // GROUP):
-                for j in range(h * GROUP, (h + 1) * GROUP):
+            for run in range(RUNS):
+                more_weights = s == 0 and run + 1 < RUNS
+                next_x = run == PREPARE_IN_RUN and s + 1 < B
+                next_att = run == PREPARE_IN_RUN and s < B
+                if more_weights:
+                    quantise(transpose_w(run + 1)[:], w_q, (run + 1) * RUN * TILE_WORDS)
+                if next_x:
+                    x_grouped = transpose_x(s + 1)
+                if next_att:
+                    att_grouped = stage.tile([P, PACK * L], BF16, tag="att_grouped", align_bytes=64)
+                    nc.scalar.copy(
+                        out=att_grouped[:].rearrange("p (c i t) -> p c t i", i=4, t=PACK),
+                        in_=att_sb[s][:].rearrange("p (t c i) -> p c t i", t=PACK, i=4),
+                    )
+                for j in range(run * RUN, (run + 1) * RUN):
                     if s < B:
                         first_matmul(x_q, j, v_grouped)
                     if s > 0:
                         second_matmul(s - 1, v_prev, att_prev, j, out_sb)
-                        if (j + 1) % STORE_TILES == 0:
-                            cols = slice((j + 1 - STORE_TILES) * L, (j + 1) * L)
-                            nc.sync.dma_start(out=out_view[:, cols], in_=out_sb[:, cols])
+                if s > 0:
+                    cols = slice(run * RUN * L, (run + 1) * RUN * L)
+                    nc.sync.dma_start(out=out_view[:, cols], in_=out_sb[:, cols])
                 if s < B:
-                    nc.vector.quantize_mx(
-                        out=v_codes[:, h * GROUP * P : (h + 1) * GROUP * P].bitcast(FP8X4),
-                        scales=v_scales[:, h * GROUP * P : (h + 1) * GROUP * P],
-                        in_=v_grouped[:, h * GROUP * BANK : (h + 1) * GROUP * BANK],
+                    quantise(
+                        v_grouped[:, run * RUN * BANK : (run + 1) * RUN * BANK], v_q, run * RUN * P
                     )
-                if h == 0 and s + 1 < B:
-                    x_next = quantise(x_grouped, stage, "x")
-                if h == 1 and s < B:
-                    att_q = quantise(att_grouped, stage, "att")
+                if next_x:
+                    x_next = mx_tiles(stage, "x", PACK * TILE_WORDS)
+                    quantise(x_grouped[:], x_next, 0)
+            if s < B:
+                att_q = mx_tiles(stage, "att", L)
+                quantise(att_grouped[:], att_q, 0)

@@ -226,6 +226,6 @@ def tile_dualcrossmodalattention_pb_kernel(tc, x, Wv1, bv1, att2, gamma2, y, out
                 if next_x:
                     x_next = mx_tiles(stage, "x", PACK * TILE_WORDS)
                     quantise(x_grouped[:], x_next, 0)
-            if s < B:
-                att_q = mx_tiles(stage, "att", L)
-                quantise(att_grouped[:], att_q, 0)
+                if next_att:
+                    att_q = mx_tiles(stage, "att", L)
+                    quantise(att_grouped[:], att_q, 0)

@@ -25,6 +25,9 @@ D_TILES = D // P
 RUN = 2
 RUNS = D_TILES // RUN
 PREPARE_IN_RUN = 2
+W_AHEAD = 2
+SCALAR_SHARE = 3
+SCALAR_SHARE_LAST = 1
 
 FLOPS = 2 * B * L * D * D + 2 * B * D * L * L
 
@@ -116,7 +119,7 @@ def tile_dualcrossmodalattention_pb_kernel(tc, x, Wv1, bv1, att2, gamma2, y, out
                 op=ADD,
             )
 
-        def second_matmul(b, v_q, att_q, j, out_sb):
+        def second_matmul(b, v_q, att_q, j, out_sb, scalar_share):
             v_codes, v_scales = operand(v_q, j * P, P)
             att_codes, att_scales = operand(att_q, 0, L)
             o_ps = psum_s.tile([P, BANK], F32, tag="bank")
@@ -130,7 +133,7 @@ def tile_dualcrossmodalattention_pb_kernel(tc, x, Wv1, bv1, att2, gamma2, y, out
                 stop=True,
             )
             cols = slice(j * L, (j + 1) * L)
-            if j % RUN == 0:
+            if j % 4 < scalar_share:
                 nc.scalar.activation(out=out_sb[:, cols], in_=o_ps[:], func=COPY, scale=gamma[:, 0:1])
                 nc.gpsimd.tensor_tensor(
                     out=out_sb[:, cols], in0=out_sb[:, cols], in1=y_sb[b][:, cols], op=ADD
@@ -153,11 +156,25 @@ def tile_dualcrossmodalattention_pb_kernel(tc, x, Wv1, bv1, att2, gamma2, y, out
             return x_grouped
 
         def transpose_w(run):
-            w_grouped = stage.tile([P, RUN * D], BF16, tag="w_grouped", align_bytes=64)
+            w_grouped = stage.tile(
+                [P, RUN * D], BF16, tag="w_grouped", bufs=W_AHEAD + 1, align_bytes=64
+            )
             for i in range(RUN):
                 j = run * RUN + i
                 transpose_tile(w_sb[:, j * D : (j + 1) * D], w_grouped[:, i * D : (i + 1) * D])
             return w_grouped
+
+        def regroup_att(b, half, att_grouped):
+            width = L // 2
+            rows = att_sb[b][:].rearrange("p (t m) -> p t m", t=PACK)
+            nc.scalar.copy(
+                out=att_grouped[:, half * width * PACK : (half + 1) * width * PACK].rearrange(
+                    "p (c i t) -> p c t i", i=4, t=PACK
+                ),
+                in_=rows[:, :, half * width : (half + 1) * width].rearrange(
+                    "p t (c i) -> p c t i", i=4
+                ),
+            )
 
         x_grouped = transpose_x(0)
         x_next = mx_tiles(stage, "x", PACK * TILE_WORDS)
@@ -183,11 +200,13 @@ def tile_dualcrossmodalattention_pb_kernel(tc, x, Wv1, bv1, att2, gamma2, y, out
         nc.vector.tensor_copy(out=gamma[:], in_=gamma_bf[:])
 
         w_q = mx_tiles(const, "w", D_TILES * TILE_WORDS)
-        quantise(transpose_w(0)[:], w_q, 0)
+        for run in range(W_AHEAD):
+            quantise(transpose_w(run)[:], w_q, run * RUN * TILE_WORDS)
 
         v_q = None
         att_q = None
         for s in range(B + 1):
+            scalar_share = SCALAR_SHARE if s < B else SCALAR_SHARE_LAST
             x_q = x_next
             v_prev = v_q
             att_prev = att_q
@@ -198,24 +217,22 @@ def tile_dualcrossmodalattention_pb_kernel(tc, x, Wv1, bv1, att2, gamma2, y, out
                 out_sb = stage.tile([P, D_TILES * L], F32, tag="out_sb")
                 out_view = out[s - 1].rearrange("(p a) c -> p (a c)", a=PACK)
             for run in range(RUNS):
-                more_weights = s == 0 and run + 1 < RUNS
                 next_x = run == PREPARE_IN_RUN and s + 1 < B
                 next_att = run == PREPARE_IN_RUN and s < B
-                if more_weights:
-                    quantise(transpose_w(run + 1)[:], w_q, (run + 1) * RUN * TILE_WORDS)
+                if s == 0 and run + W_AHEAD < RUNS:
+                    quantise(transpose_w(run + W_AHEAD)[:], w_q, (run + W_AHEAD) * RUN * TILE_WORDS)
                 if next_x:
                     x_grouped = transpose_x(s + 1)
-                if next_att:
+                if s < B and run == PREPARE_IN_RUN - 1:
                     att_grouped = stage.tile([P, PACK * L], BF16, tag="att_grouped", align_bytes=64)
-                    nc.scalar.copy(
-                        out=att_grouped[:].rearrange("p (c i t) -> p c t i", i=4, t=PACK),
-                        in_=att_sb[s][:].rearrange("p (t c i) -> p c t i", t=PACK, i=4),
-                    )
+                    regroup_att(s, 0, att_grouped)
+                if next_att:
+                    regroup_att(s, 1, att_grouped)
                 for j in range(run * RUN, (run + 1) * RUN):
                     if s < B:
                         first_matmul(x_q, j, v_grouped)
                     if s > 0:
-                        second_matmul(s - 1, v_prev, att_prev, j, out_sb)
+                        second_matmul(s - 1, v_prev, att_prev, j, out_sb, scalar_share)
                 if s > 0:
                     cols = slice(run * RUN * L, (run + 1) * RUN * L)
                     nc.sync.dma_start(out=out_view[:, cols], in_=out_sb[:, cols])

@@ -24,10 +24,12 @@ TILE_WORDS = D // PACK
 D_TILES = D // P
 RUN = 2
 RUNS = D_TILES // RUN
-PREPARE_IN_RUN = 2
 W_AHEAD = 2
-SCALAR_SHARE = 3
-SCALAR_SHARE_LAST = 1
+X1_BEFORE_TILE = 4
+ATT_BEFORE_TILE = 5
+X_QUANTISED_AFTER_TILE = 5
+SECOND_LAG = 1
+SCALAR_TILES = 3
 
 FLOPS = 2 * B * L * D * D + 2 * B * D * L * L
 
@@ -119,7 +121,7 @@ def tile_dualcrossmodalattention_pb_kernel(tc, x, Wv1, bv1, att2, gamma2, y, out
                 op=ADD,
             )
 
-        def second_matmul(b, v_q, att_q, j, out_sb, scalar_share):
+        def second_matmul(b, v_q, att_q, j, out_sb, through_scalar):
             v_codes, v_scales = operand(v_q, j * P, P)
             att_codes, att_scales = operand(att_q, 0, L)
             o_ps = psum_s.tile([P, BANK], F32, tag="bank")
@@ -133,7 +135,7 @@ def tile_dualcrossmodalattention_pb_kernel(tc, x, Wv1, bv1, att2, gamma2, y, out
                 stop=True,
             )
             cols = slice(j * L, (j + 1) * L)
-            if j % 4 < scalar_share:
+            if through_scalar:
                 nc.scalar.activation(out=out_sb[:, cols], in_=o_ps[:], func=COPY, scale=gamma[:, 0:1])
                 nc.gpsimd.tensor_tensor(
                     out=out_sb[:, cols], in0=out_sb[:, cols], in1=y_sb[b][:, cols], op=ADD
@@ -164,17 +166,13 @@ def tile_dualcrossmodalattention_pb_kernel(tc, x, Wv1, bv1, att2, gamma2, y, out
                 transpose_tile(w_sb[:, j * D : (j + 1) * D], w_grouped[:, i * D : (i + 1) * D])
             return w_grouped
 
-        def regroup_att(b, half, att_grouped):
-            width = L // 2
-            rows = att_sb[b][:].rearrange("p (t m) -> p t m", t=PACK)
+        def regroup_att(b):
+            att_grouped = stage.tile([P, PACK * L], BF16, tag="att_grouped", align_bytes=64)
             nc.scalar.copy(
-                out=att_grouped[:, half * width * PACK : (half + 1) * width * PACK].rearrange(
-                    "p (c i t) -> p c t i", i=4, t=PACK
-                ),
-                in_=rows[:, :, half * width : (half + 1) * width].rearrange(
-                    "p t (c i) -> p c t i", i=4
-                ),
+                out=att_grouped[:].rearrange("p (c i t) -> p c t i", i=4, t=PACK),
+                in_=att_sb[b][:].rearrange("p (t c i) -> p c t i", t=PACK, i=4),
             )
+            return att_grouped
 
         x_grouped = transpose_x(0)
         x_next = mx_tiles(stage, "x", PACK * TILE_WORDS)
@@ -206,43 +204,37 @@ def tile_dualcrossmodalattention_pb_kernel(tc, x, Wv1, bv1, att2, gamma2, y, out
         v_q = None
         att_q = None
         for s in range(B + 1):
-            scalar_share = SCALAR_SHARE if s < B else SCALAR_SHARE_LAST
             x_q = x_next
             v_prev = v_q
             att_prev = att_q
             if s < B:
                 v_grouped = stage.tile([P, D_TILES * BANK], BF16, tag="v_grouped", align_bytes=64)
-                v_q = mx_tiles(stage, "v", D_TILES * P)
             if s > 0:
                 out_sb = stage.tile([P, D_TILES * L], F32, tag="out_sb")
                 out_view = out[s - 1].rearrange("(p a) c -> p (a c)", a=PACK)
-            for run in range(RUNS):
-                next_x = run == PREPARE_IN_RUN and s + 1 < B
-                next_att = run == PREPARE_IN_RUN and s < B
-                if s == 0 and run + W_AHEAD < RUNS:
-                    quantise(transpose_w(run + W_AHEAD)[:], w_q, (run + W_AHEAD) * RUN * TILE_WORDS)
-                if next_x:
+            for i in range(D_TILES):
+                w_run = i // RUN + W_AHEAD
+                if s == 0 and i % RUN == 0 and w_run < RUNS:
+                    quantise(transpose_w(w_run)[:], w_q, w_run * RUN * TILE_WORDS)
+                if s + 1 < B and i == (X1_BEFORE_TILE if s == 0 else 0):
                     x_grouped = transpose_x(s + 1)
-                if s < B and run == PREPARE_IN_RUN - 1:
-                    att_grouped = stage.tile([P, PACK * L], BF16, tag="att_grouped", align_bytes=64)
-                    regroup_att(s, 0, att_grouped)
-                if next_att:
-                    regroup_att(s, 1, att_grouped)
-                for j in range(run * RUN, (run + 1) * RUN):
-                    if s < B:
-                        first_matmul(x_q, j, v_grouped)
-                    if s > 0:
-                        second_matmul(s - 1, v_prev, att_prev, j, out_sb, scalar_share)
-                if s > 0:
-                    cols = slice(run * RUN * L, (run + 1) * RUN * L)
-                    nc.sync.dma_start(out=out_view[:, cols], in_=out_sb[:, cols])
+                if s < B and i == ATT_BEFORE_TILE:
+                    att_grouped = regroup_att(s)
                 if s < B:
-                    quantise(
-                        v_grouped[:, run * RUN * BANK : (run + 1) * RUN * BANK], v_q, run * RUN * P
-                    )
-                if next_x:
+                    first_matmul(x_q, i, v_grouped)
+                o_run = i - SECOND_LAG
+                if s > 0 and 0 <= o_run < RUNS:
+                    for j in range(o_run * RUN, (o_run + 1) * RUN):
+                        second_matmul(s - 1, v_prev, att_prev, j, out_sb, s < B and j < SCALAR_TILES)
+                    cols = slice(o_run * RUN * L, (o_run + 1) * RUN * L)
+                    nc.sync.dma_start(out=out_view[:, cols], in_=out_sb[:, cols])
+                if s + 1 < B and i == X_QUANTISED_AFTER_TILE:
                     x_next = mx_tiles(stage, "x", PACK * TILE_WORDS)
                     quantise(x_grouped[:], x_next, 0)
-                if next_att:
-                    att_q = mx_tiles(stage, "att", L)
-                    quantise(att_grouped[:], att_q, 0)
+            if s < B:
+                half = D_TILES * BANK // 2
+                v_q = mx_tiles(stage, "v", D_TILES * P)
+                att_q = mx_tiles(stage, "att", L)
+                quantise(v_grouped[:, :half], v_q, 0)
+                quantise(att_grouped[:], att_q, 0)
+                quantise(v_grouped[:, half:], v_q, half // PACK)

@@ -25,11 +25,12 @@ D_TILES = D // P
 RUN = 2
 RUNS = D_TILES // RUN
 W_AHEAD = 2
-X1_BEFORE_TILE = 4
-ATT_BEFORE_TILE = 5
-X_QUANTISED_AFTER_TILE = 5
-SECOND_LAG = 1
-SCALAR_TILES = 3
+PLANS = [
+    "W0 w1 w2 W1 w3 m00 m01 W2 d00 m02 d01 W3 m03 t1 d02 m04 d03 m05 d04 m06 d05 r0 x1 q004 m07 d06 d07 a0 q048 t2 m10 m11 m12",
+    "S00 S01 S02 S03 o002 o024 d10 d11 d12 D04 m13 d13 D05 o046 D06 m14 d14 D07 o068 r1 m15 m16 m17 d15 d16 t3 x2 q104 d17 a1 q148 m20 m21 m22",
+    "S10 S11 S12 S13 o102 o124 d20 d21 d22 D14 m23 d23 D15 o146 D16 m24 d24 D17 o168 r2 m25 m26 m27 d25 d26  x3 q204 d27 a2 q248 m30 m31 m32 r3",
+    "S20 S21 S22 S23 o202 o224 d30 d31 d32 D24 m33 d33 D25 o246 D26 m34 d34 D27 o268 m35 m36 m37 a3 q304 d35 S30 d36 D31 d37 D32 q348 D33 o302 o324 D34 D35 o346 D36 o367 D37 o378",
+]
 
 FLOPS = 2 * B * L * D * D + 2 * B * D * L * L
 
@@ -51,37 +52,43 @@ def tile_dualcrossmodalattention_pb_kernel(tc, x, Wv1, bv1, att2, gamma2, y, out
         bias_row = const.tile([P, D], BF16)
         nc.vector.memset(bias_row[:], 0.0)
 
-        def load(pool, tag, rows_view, pieces):
+        def load(pool, tag, rows_view, pieces, bias_after=-1):
             width = rows_view.shape[1]
             landed = pool.tile([P, width], BF16, tag=tag)
             for piece in range(pieces):
                 cols = slice(piece * width // pieces, (piece + 1) * width // pieces)
                 nc.sync.dma_start(out=landed[:, cols], in_=rows_view[:, cols])
+                if piece == bias_after:
+                    nc.sync.dma_start(out=bias_row[0:1, :], in_=bv1.unsqueeze(0))
             return landed
 
-        def load_x(b, pieces):
-            return load(loads, "x", x[b].rearrange("(p t) k -> p (t k)", t=PACK), pieces)
+        def load_x(b, pieces, bias_after=-1):
+            return load(loads, "x", x[b].rearrange("(p t) k -> p (t k)", t=PACK), pieces, bias_after)
 
-        x_sb = [load_x(0, PACK)]
-        nc.sync.dma_start(out=bias_row[0:1, :], in_=bv1.unsqueeze(0))
+        x_sb = [load_x(0, PACK, bias_after=1)]
         gamma_bf = const.tile([P, 1], BF16)
         nc.sync.dma_start(out=gamma_bf[:], in_=gamma2.partition_broadcast(P))
         w_sb = load(const, "w", Wv1.rearrange("(p j) k -> p (j k)", j=D_TILES), RUNS)
-        att_sb = []
-        y_sb = []
-        for b in range(B):
-            if b + 1 < B:
-                x_sb.append(load_x(b + 1, 1))
-            att_sb.append(load(loads, "att", att2[b].rearrange("(p t) m -> p (t m)", t=PACK), 1))
-            y_sb.append(load(loads, "y", y[b].rearrange("(p a) c -> p (a c)", a=PACK), 1))
+        att_sb = {}
+        y_sb = {}
+        x_sb = {0: x_sb[0]}
+        for word in "x1 a0 x2 y0 a1 x3 y1 a2 y2 a3 y3".split():
+            b = int(word[1])
+            if word[0] == "x":
+                x_sb[b] = load_x(b, 1)
+            elif word[0] == "a":
+                att_sb[b] = load(loads, "att", att2[b].rearrange("(p t) m -> p (t m)", t=PACK), 1)
+            else:
+                y_sb[b] = load(loads, "y", y[b].rearrange("(p a) c -> p (a c)", a=PACK), 1)
 
-        def transpose_tile(rows, grouped):
+        def transpose_tile(rows, grouped, through_vector=False):
             bank = psum_s.tile([P, BANK], F32, tag="bank")
             words = rows.bitcast(F32)
             for chunk in range(BANK // P):
                 cols = slice(chunk * P, (chunk + 1) * P)
                 nc.tensor.transpose(bank[:, cols], words[:, cols], ident[:])
-            nc.scalar.copy(
+            copy = nc.vector.tensor_copy if through_vector else nc.scalar.copy
+            copy(
                 out=grouped.bitcast(F32).rearrange("p (g r u) -> p g r u", g=PASSES, u=2),
                 in_=bank[:].rearrange("p (g u r) -> p g r u", g=PASSES, u=2),
             )
@@ -99,8 +106,8 @@ def tile_dualcrossmodalattention_pb_kernel(tc, x, Wv1, bv1, att2, gamma2, y, out
             codes, scales = operand(mx, first, grouped.shape[1] // PACK)
             nc.vector.quantize_mx(out=codes, scales=scales, in_=grouped)
 
-        def first_matmul(x_q, j, v_grouped):
-            v_ps = psum_v.tile([P, BANK], F32)
+        def first_matmul(x_q, j):
+            v_ps = psum_v.tile([P, BANK], F32, tag="v_ps")
             for t in range(PACK):
                 for g in range(PASSES):
                     x_codes, x_scales = operand(x_q, t * TILE_WORDS + g * P, P)
@@ -114,6 +121,9 @@ def tile_dualcrossmodalattention_pb_kernel(tc, x, Wv1, bv1, att2, gamma2, y, out
                         start=(g == 0),
                         stop=(g == PASSES - 1),
                     )
+            return v_ps
+
+        def first_drain(v_ps, j, v_grouped):
             nc.vector.tensor_tensor(
                 out=v_grouped[:, j * BANK : (j + 1) * BANK].rearrange("p (r t) -> p r t", t=PACK),
                 in0=v_ps[:].rearrange("p (t r) -> p r t", t=PACK),
@@ -150,20 +160,20 @@ def tile_dualcrossmodalattention_pb_kernel(tc, x, Wv1, bv1, att2, gamma2, y, out
                     op1=ADD,
                 )
 
-        def transpose_x(b):
+        def transpose_x(b, vector_tiles=()):
             x_grouped = stage.tile([P, PACK * D], BF16, tag="x_grouped", align_bytes=64)
             for t in range(PACK):
                 cols = slice(t * D, (t + 1) * D)
-                transpose_tile(x_sb[b][:, cols], x_grouped[:, cols])
+                transpose_tile(x_sb[b][:, cols], x_grouped[:, cols], t in vector_tiles)
             return x_grouped
 
-        def transpose_w(run):
+        def transpose_w(run, vector_tiles=()):
             w_grouped = stage.tile(
                 [P, RUN * D], BF16, tag="w_grouped", bufs=W_AHEAD + 1, align_bytes=64
             )
             for i in range(RUN):
                 j = run * RUN + i
-                transpose_tile(w_sb[:, j * D : (j + 1) * D], w_grouped[:, i * D : (i + 1) * D])
+                transpose_tile(w_sb[:, j * D : (j + 1) * D], w_grouped[:, i * D : (i + 1) * D], j in vector_tiles)
             return w_grouped
 
         def regroup_att(b):
@@ -174,14 +184,15 @@ def tile_dualcrossmodalattention_pb_kernel(tc, x, Wv1, bv1, att2, gamma2, y, out
             )
             return att_grouped
 
-        x_grouped = transpose_x(0)
-        x_next = mx_tiles(stage, "x", PACK * TILE_WORDS)
+        x_grouped = transpose_x(0, vector_tiles=())
+        x_q = mx_tiles(stage, "x", PACK * TILE_WORDS)
         for t in range(PACK):
-            quantise(x_grouped[:, t * D : (t + 1) * D], x_next, t * TILE_WORDS)
-
+            quantise(x_grouped[:, t * D : (t + 1) * D], x_q, t * TILE_WORDS)
+        w_q = mx_tiles(const, "w", D_TILES * TILE_WORDS)
+        w_grouped = [transpose_w(0)]
         bias_by_tile = const.tile([P, D_TILES, P], F32)
         for half in range(D // BANK):
-            bias_ps = psum_s.tile([P, BANK], F32, tag="bank")
+            bias_ps = psum_v.tile([P, BANK], F32, tag="v_ps")
             nc.tensor.matmul(
                 bias_ps[:],
                 lhsT=ones[:],
@@ -197,44 +208,62 @@ def tile_dualcrossmodalattention_pb_kernel(tc, x, Wv1, bv1, att2, gamma2, y, out
         gamma = const.tile([P, 1], F32)
         nc.vector.tensor_copy(out=gamma[:], in_=gamma_bf[:])
 
-        w_q = mx_tiles(const, "w", D_TILES * TILE_WORDS)
-        for run in range(W_AHEAD):
-            quantise(transpose_w(run)[:], w_q, run * RUN * TILE_WORDS)
+        def quantise_w(run):
+            quantise(w_grouped[run][:], w_q, run * RUN * TILE_WORDS)
 
-        v_q = None
-        att_q = None
-        for s in range(B + 1):
-            x_q = x_next
-            v_prev = v_q
-            att_prev = att_q
-            if s < B:
-                v_grouped = stage.tile([P, D_TILES * BANK], BF16, tag="v_grouped", align_bytes=64)
-            if s > 0:
-                out_sb = stage.tile([P, D_TILES * L], F32, tag="out_sb")
-                out_view = out[s - 1].rearrange("(p a) c -> p (a c)", a=PACK)
-            for i in range(D_TILES):
-                w_run = i // RUN + W_AHEAD
-                if s == 0 and i % RUN == 0 and w_run < RUNS:
-                    quantise(transpose_w(w_run)[:], w_q, w_run * RUN * TILE_WORDS)
-                if s + 1 < B and i == (X1_BEFORE_TILE if s == 0 else 0):
-                    x_grouped = transpose_x(s + 1)
-                if s < B and i == ATT_BEFORE_TILE:
-                    att_grouped = regroup_att(s)
-                if s < B:
-                    first_matmul(x_q, i, v_grouped)
-                o_run = i - SECOND_LAG
-                if s > 0 and 0 <= o_run < RUNS:
-                    for j in range(o_run * RUN, (o_run + 1) * RUN):
-                        second_matmul(s - 1, v_prev, att_prev, j, out_sb, s < B and j < SCALAR_TILES)
-                    cols = slice(o_run * RUN * L, (o_run + 1) * RUN * L)
-                    nc.sync.dma_start(out=out_view[:, cols], in_=out_sb[:, cols])
-                if s + 1 < B and i == X_QUANTISED_AFTER_TILE:
-                    x_next = mx_tiles(stage, "x", PACK * TILE_WORDS)
-                    quantise(x_grouped[:], x_next, 0)
-            if s < B:
-                half = D_TILES * BANK // 2
-                v_q = mx_tiles(stage, "v", D_TILES * P)
-                att_q = mx_tiles(stage, "att", L)
-                quantise(v_grouped[:, :half], v_q, 0)
-                quantise(att_grouped[:], att_q, 0)
-                quantise(v_grouped[:, half:], v_q, half // PACK)
+        HALF = D_TILES * BANK // 2
+        v_grouped = {}
+        v_ps = {}
+        v_q = {}
+        att_grouped = {}
+        att_q = {}
+        out_sb = {}
+        x_grouped = {}
+        x_mx = {0: x_q}
+
+        def run_plan(plan):
+            for word in plan.split():
+                kind, b, arg = word[0], int(word[1]), word[2:]
+                if kind == "w":
+                    w_grouped.append(transpose_w(b, vector_tiles=()))
+                elif kind == "W":
+                    quantise_w(b)
+                elif kind == "t":
+                    x_grouped[b] = transpose_x(b)
+                elif kind == "r":
+                    att_grouped[b] = regroup_att(b)
+                elif kind == "x":
+                    x_mx[b] = mx_tiles(stage, "x", PACK * TILE_WORDS)
+                    quantise(x_grouped[b][:], x_mx[b], 0)
+                elif kind == "a":
+                    att_q[b] = mx_tiles(stage, "att", L)
+                    quantise(att_grouped[b][:], att_q[b], 0)
+                elif kind == "q":
+                    first, last = int(arg[0]), int(arg[1])
+                    if first == 0:
+                        v_q[b] = mx_tiles(stage, "v", D_TILES * P)
+                    quantise(v_grouped[b][:, first * BANK : last * BANK], v_q[b], first * P)
+                elif kind == "v":
+                    if arg == "0":
+                        v_tile = stage.tile([P, D_TILES * BANK], BF16, tag="v_grouped", align_bytes=64)
+                        v_grouped[b] = v_tile
+                    first_drain(first_matmul(x_mx[b], int(arg)), int(arg), v_grouped[b])
+                elif kind == "m":
+                    v_ps[b, int(arg)] = first_matmul(x_mx[b], int(arg))
+                elif kind == "d":
+                    if arg == "0":
+                        v_tile = stage.tile([P, D_TILES * BANK], BF16, tag="v_grouped", align_bytes=64)
+                        v_grouped[b] = v_tile
+                    first_drain(v_ps[b, int(arg)], int(arg), v_grouped[b])
+                elif kind in "SD":
+                    j = int(arg)
+                    if j == 0:
+                        out_tile = stage.tile([P, D_TILES * L], F32, tag="out_sb")
+                        out_sb[b] = out_tile
+                    second_matmul(b, v_q[b], att_q[b], j, out_sb[b], kind == "S")
+                elif kind == "o":
+                    cols = slice(int(arg[0]) * L, int(arg[1]) * L)
+                    nc.sync.dma_start(out=out[b].rearrange("(p a) c -> p (a c)", a=PACK)[:, cols], in_=out_sb[b][:, cols])
+
+        for plan in PLANS:
+            run_plan(plan)

@@ -27,8 +27,8 @@ RUNS = D_TILES // RUN
 W_AHEAD = 2
 PLANS = [
     "W0 w1 w2 W1 w3 m00 m01 W2 d00 m02 d01 W3 m03 t1 d02 m04 d03 m05 d04 m06 d05 r0 x1 q004 m07 d06 d07 a0 q048 t2 m10 m11 m12",
-    "S00 S01 S02 S03 o002 o024 d10 d11 d12 D04 m13 d13 D05 o046 D06 m14 d14 D07 o068 r1 m15 m16 m17 d15 d16 t3 x2 q104 d17 a1 q148 m20 m21 m22",
-    "S10 S11 S12 S13 o102 o124 d20 d21 d22 D14 m23 d23 D15 o146 D16 m24 d24 D17 o168 r2 m25 m26 m27 d25 d26  x3 q204 d27 a2 q248 m30 m31 m32 r3",
+    "S00 S01 S02 S03 o002 o024 d10 d11 d12 D04 m13 d13 S05 o046 D06 m14 d14 D07 o068 r1 m15 m16 m17 d15 d16 t3 x2 q104 d17 a1 q148 m20 m21 m22",
+    "S10 S11 S12 S13 o102 o124 d20 d21 d22 D14 m23 d23 S15 o146 D16 m24 d24 D17 o168 r2 m25 m26 m27 d25 d26  x3 q204 d27 a2 q248 m30 m31 m32 r3",
     "S20 S21 S22 S23 o202 o224 d30 d31 d32 D24 m33 d33 D25 o246 D26 m34 d34 D27 o268 m35 m36 m37 a3 q304 d35 S30 d36 D31 d37 D32 q348 D33 o302 o324 D34 D35 o346 D36 o367 D37 o378",
 ]
 

@@ -28,8 +28,8 @@ W_AHEAD = 2
 PLANS = [
     "W0 w1 w2 W1 w3 m00 m01 W2 d00 m02 d01 W3 m03 t1 d02 m04 d03 m05 d04 m06 d05 r0 x1 q004 m07 d06 d07 a0 q048 t2 m10 m11 m12",
     "S00 S01 S02 S03 o002 o024 d10 d11 d12 D04 m13 d13 S05 o046 D06 m14 d14 D07 o068 r1 m15 m16 m17 d15 d16 t3 x2 q104 d17 a1 q148 m20 m21 m22",
-    "S10 S11 S12 S13 o102 o124 d20 d21 d22 D14 m23 d23 S15 o146 D16 m24 d24 D17 o168 r2 m25 m26 m27 d25 d26  x3 q204 d27 a2 q248 m30 m31 m32 r3",
-    "S20 S21 S22 S23 o202 o224 d30 d31 d32 D24 m33 d33 D25 o246 D26 m34 d34 D27 o268 m35 m36 m37 a3 q304 d35 S30 d36 D31 d37 D32 q348 D33 o302 o324 D34 D35 o346 D36 o367 D37 o378",
+    "S10 S11 S12 S13 o102 o124 d20 d21 d22 D14 m23 d23 S15 o146 D16 m24 d24 D17 o168 r2 m25 m26 m27 d25 d26  z5 x3 q204 d27 a2 q248 m30 m31 m32 r3",
+    "S20 S21 S22 S23 o202 o224 d30 d31 d32 D24 m33 d33 D25 o246 D26 m34 d34 D27 o268 m35 m36 m37 z5 a3 q304 d35 S30 d36 D31 d37 D32 q348 D33 y4 o302 o324 D34 D35 o346 D36 o367 D37 o378",
 ]
 
 FLOPS = 2 * B * L * D * D + 2 * B * D * L * L
@@ -255,6 +255,11 @@ def tile_dualcrossmodalattention_pb_kernel(tc, x, Wv1, bv1, att2, gamma2, y, out
                         v_tile = stage.tile([P, D_TILES * BANK], BF16, tag="v_grouped", align_bytes=64)
                         v_grouped[b] = v_tile
                     first_drain(v_ps[b, int(arg)], int(arg), v_grouped[b])
+                elif kind in "zy":
+                    for i in range(b):
+                        pool, tag = (psum_s, "bank") if kind == "z" else (psum_v, "v_ps")
+                        idle = pool.tile([P, BANK], F32, tag=tag)
+                        nc.tensor.matmul(idle[:], lhsT=ones[:], rhs=bias_row[:, :BANK], start=True, stop=True)
                 elif kind in "SD":
                     j = int(arg)
                     if j == 0:

@@ -26,12 +26,13 @@ RUN = 2
 RUNS = D_TILES // RUN
 W_AHEAD = 2
 PLANS = [
-    "W0 w1 w2 W1 w3 m00 m01 W2 d00 m02 d01 W3 m03 t1 d02 m04 d03 m05 d04 m06 d05 r0 x1 q004 m07 d06 d07 a0 q048 t2 m10 m11 m12",
-    "S00 S01 S02 S03 o002 o024 d10 d11 d12 D04 m13 d13 S05 o046 D06 m14 d14 D07 o068 r1 m15 m16 m17 d15 d16 t3 x2 q104 d17 a1 q148 m20 m21 m22",
-    "S10 S11 S12 S13 o102 o124 d20 d21 d22 D14 m23 d23 S15 o146 D16 m24 d24 D17 o168 r2 m25 m26 m27 d25 d26  z5 x3 q204 d27 a2 q248 m30 m31 m32 r3",
-    "S20 S21 S22 S23 o202 o224 d30 d31 d32 D24 m33 d33 D25 o246 D26 m34 d34 D27 o268 m35 m36 m37 z5 a3 q304 d35 S30 d36 D31 d37 D32 q348 D33 y4 o302 o324 D34 D35 o346 D36 o367 D37 o378",
+    "W0 w1 w2 W1 w3 m00 m01 W2 d00 m02 d01 W3 m03 t1 d02 m04 d03 m05 q004 d04 m06 d05 r0 x1 m07 d06 d07 a0 t2 m10 m11 S00 S01 q048 m12",
+    "d10 d11 S02 S03 d12 D05 m13 d13 S04 D06 m14 d14 D07 o056 o002 o068 o024 o045 r1 m15 m16 m17 d15 d16 t3 d17 x2 q104 a1 m20 m21 S10 S11 q148 m22",
+    "d20 d21 S12 S13 d22 D15 m23 d23 S14 D16 m24 d24 D17 o156 o102 o168 o124 o145 r2 m25 m26 m27 d25 d26  d27 r3 z4 x3 q204 a2 m30 m31 S20 S21 q248 m32",
+    "d30 d31 S22 S23 d32 D24 m33 d33 D25 D26 m34 d34 D27 o246 o202 o268 o224 m35 m36 d35 a3 q304 m37 d36 z3 d37 D30 D31 o302 q348 y3 D32 D33 o324 D34 D35 o346 D36 o367 D37 o378",
 ]
 
+WARM = 16
 FLOPS = 2 * B * L * D * D + 2 * B * D * L * L
 
 
@@ -184,12 +185,14 @@ def tile_dualcrossmodalattention_pb_kernel(tc, x, Wv1, bv1, att2, gamma2, y, out
             )
             return att_grouped
 
+        for i in range(WARM):
+            idle = psum_v.tile([P, BANK], F32, tag="v_ps")
+            nc.tensor.matmul(idle[:, :P], lhsT=ones[:], rhs=ones[:], start=True, stop=True)
         x_grouped = transpose_x(0, vector_tiles=())
         x_q = mx_tiles(stage, "x", PACK * TILE_WORDS)
         for t in range(PACK):
             quantise(x_grouped[:, t * D : (t + 1) * D], x_q, t * TILE_WORDS)
         w_q = mx_tiles(const, "w", D_TILES * TILE_WORDS)
-        w_grouped = [transpose_w(0)]
         bias_by_tile = const.tile([P, D_TILES, P], F32)
         for half in range(D // BANK):
             bias_ps = psum_v.tile([P, BANK], F32, tag="v_ps")
@@ -205,6 +208,7 @@ def tile_dualcrossmodalattention_pb_kernel(tc, x, Wv1, bv1, att2, gamma2, y, out
                 out=bias_by_tile[:, :, half * rows : (half + 1) * rows],
                 in_=bias_ps[:].rearrange("p (r j) -> p j r", j=D_TILES),
             )
+        w_grouped = [transpose_w(0)]
         gamma = const.tile([P, 1], F32)
         nc.vector.tensor_copy(out=gamma[:], in_=gamma_bf[:])
 

@@ -26,7 +26,7 @@ RUN = 2
 RUNS = D_TILES // RUN
 W_AHEAD = 2
 PLANS = [
-    "W0 w1 w2 W1 w3 m00 m01 W2 d00 m02 d01 W3 m03 t1 d02 m04 d03 m05 q004 d04 m06 d05 r0 x1 m07 d06 d07 a0 t2 m10 m11 S00 S01 q048 m12",
+    "W0 w1 w2 W1 w3 m00 m01 W2 d00 m02 d01 W3 m03 t1 d02 m04 d03 m05 q004 d04 m06 d05 r0 x1 m07 d06 d07 g0 a0 t2 m10 m11 S00 S01 q048 m12",
     "d10 d11 S02 S03 d12 D05 m13 d13 S04 D06 m14 d14 D07 o056 o002 o068 o024 o045 r1 m15 m16 m17 d15 d16 t3 d17 x2 q104 a1 m20 m21 S10 S11 q148 m22",
     "d20 d21 S12 S13 d22 D15 m23 d23 S14 D16 m24 d24 D17 o156 o102 o168 o124 o145 r2 m25 m26 m27 d25 d26  d27 r3 z4 x3 q204 a2 m30 m31 S20 S21 q248 m32",
     "d30 d31 S22 S23 d32 D24 m33 d33 D25 D26 m34 d34 D27 o246 o202 o268 o224 m35 m36 d35 a3 q304 m37 d36 z3 d37 D30 D31 o302 q348 y3 D32 D33 o324 D34 D35 o346 D36 o367 D37 o378",
@@ -68,14 +68,15 @@ def tile_dualcrossmodalattention_pb_kernel(tc, x, Wv1, bv1, att2, gamma2, y, out
 
         x_sb = [load_x(0, PACK, bias_after=1)]
         gamma_bf = const.tile([P, 1], BF16)
-        nc.sync.dma_start(out=gamma_bf[:], in_=gamma2.partition_broadcast(P))
         w_sb = load(const, "w", Wv1.rearrange("(p j) k -> p (j k)", j=D_TILES), RUNS)
         att_sb = {}
         y_sb = {}
         x_sb = {0: x_sb[0]}
-        for word in "x1 a0 x2 y0 a1 x3 y1 a2 y2 a3 y3".split():
+        for word in "x1 a0 g0 x2 y0 a1 x3 y1 a2 y2 a3 y3".split():
             b = int(word[1])
-            if word[0] == "x":
+            if word[0] == "g":
+                nc.sync.dma_start(out=gamma_bf[:], in_=gamma2.partition_broadcast(P))
+            elif word[0] == "x":
                 x_sb[b] = load_x(b, 1)
             elif word[0] == "a":
                 att_sb[b] = load(loads, "att", att2[b].rearrange("(p t) m -> p (t m)", t=PACK), 1)
@@ -210,7 +211,6 @@ def tile_dualcrossmodalattention_pb_kernel(tc, x, Wv1, bv1, att2, gamma2, y, out
             )
         w_grouped = [transpose_w(0)]
         gamma = const.tile([P, 1], F32)
-        nc.vector.tensor_copy(out=gamma[:], in_=gamma_bf[:])
 
         def quantise_w(run):
             quantise(w_grouped[run][:], w_q, run * RUN * TILE_WORDS)
@@ -228,7 +228,9 @@ def tile_dualcrossmodalattention_pb_kernel(tc, x, Wv1, bv1, att2, gamma2, y, out
         def run_plan(plan):
             for word in plan.split():
                 kind, b, arg = word[0], int(word[1]), word[2:]
-                if kind == "w":
+                if kind == "g":
+                    nc.vector.tensor_copy(out=gamma[:], in_=gamma_bf[:])
+                elif kind == "w":
                     w_grouped.append(transpose_w(b, vector_tiles=()))
                 elif kind == "W":
                     quantise_w(b)

from contextlib import ExitStack

import concourse.mybir as mybir
from concourse.masks import make_identity

F32 = mybir.dt.float32
BF16 = mybir.dt.bfloat16
U32 = mybir.dt.uint32
U8 = mybir.dt.uint8
FP8X4 = mybir.dt.float8_e4m3fn_x4
ADD = mybir.AluOpType.add
MULT = mybir.AluOpType.mult
COPY = mybir.ActivationFunctionType.Copy

P = 128
PACK = 4
K_PASS = P * PACK
B = 4
L = 512
D = 1024
BANK = 512
PASSES = D // K_PASS
TILE_WORDS = D // PACK
D_TILES = D // P
RUN = 2
RUNS = D_TILES // RUN
W_AHEAD = 2
PLANS = [
    "W0 w1 w2 W1 w3 m00 m01 W2 d00 m02 d01 W3 m03 t1 d02 m04 d03 m05 q004 d04 m06 d05 r0 x1 m07 d06 d07 g0 a0 t2 m10 m11 S00 S01 q048 m12",
    "d10 d11 S02 S03 d12 D05 m13 d13 S04 D06 m14 d14 D07 o056 o002 o068 o024 o045 r1 m15 m16 m17 d15 d16 t3 d17 x2 q104 a1 m20 m21 S10 S11 q148 m22",
    "d20 d21 S12 S13 d22 D15 m23 d23 S14 D16 m24 d24 D17 o156 o102 o168 o124 o145 r2 m25 m26 m27 d25 d26  d27 r3 z4 x3 q204 a2 m30 m31 S20 S21 q248 m32",
    "d30 d31 S22 S23 d32 D24 m33 d33 D25 D26 m34 d34 D27 o246 o202 o268 o224 m35 m36 d35 a3 q304 m37 d36 z3 d37 D30 D31 o302 q348 y3 D32 D33 o324 D34 D35 o346 D36 o367 D37 o378",
]

WARM = 16
FLOPS = 2 * B * L * D * D + 2 * B * D * L * L


def tile_dualcrossmodalattention_pb_kernel(tc, x, Wv1, bv1, att2, gamma2, y, out):
    nc = tc.nc
    with ExitStack() as ctx:
        ctx.enter_context(tc.manual_schedule())
        const = ctx.enter_context(tc.tile_pool(name="const", bufs=1))
        loads = ctx.enter_context(tc.tile_pool(name="loads", bufs=B))
        stage = ctx.enter_context(tc.tile_pool(name="stage", bufs=2))
        psum_v = ctx.enter_context(tc.psum_pool(name="psum_v", bufs=3))
        psum_s = ctx.enter_context(tc.psum_pool(name="psum_s", bufs=5))

        ident = const.tile([P, P], F32)
        make_identity(nc, ident[:])
        ones = const.tile([P, P], BF16)
        nc.vector.memset(ones[:], 1.0)
        bias_row = const.tile([P, D], BF16)
        nc.vector.memset(bias_row[:], 0.0)

        def load(pool, tag, rows_view, pieces, bias_after=-1):
            width = rows_view.shape[1]
            landed = pool.tile([P, width], BF16, tag=tag)
            for piece in range(pieces):
                cols = slice(piece * width // pieces, (piece + 1) * width // pieces)
                nc.sync.dma_start(out=landed[:, cols], in_=rows_view[:, cols])
                if piece == bias_after:
                    nc.sync.dma_start(out=bias_row[0:1, :], in_=bv1.unsqueeze(0))
            return landed

        def load_x(b, pieces, bias_after=-1):
            return load(loads, "x", x[b].rearrange("(p t) k -> p (t k)", t=PACK), pieces, bias_after)

        x_sb = [load_x(0, PACK, bias_after=1)]
        gamma_bf = const.tile([P, 1], BF16)
        w_sb = load(const, "w", Wv1.rearrange("(p j) k -> p (j k)", j=D_TILES), RUNS)
        att_sb = {}
        y_sb = {}
        x_sb = {0: x_sb[0]}
        for word in "x1 a0 g0 x2 y0 a1 x3 y1 a2 y2 a3 y3".split():
            b = int(word[1])
            if word[0] == "g":
                nc.sync.dma_start(out=gamma_bf[:], in_=gamma2.partition_broadcast(P))
            elif word[0] == "x":
                x_sb[b] = load_x(b, 1)
            elif word[0] == "a":
                att_sb[b] = load(loads, "att", att2[b].rearrange("(p t) m -> p (t m)", t=PACK), 1)
            else:
                y_sb[b] = load(loads, "y", y[b].rearrange("(p a) c -> p (a c)", a=PACK), 1)

        def transpose_tile(rows, grouped, through_vector=False):
            bank = psum_s.tile([P, BANK], F32, tag="bank")
            words = rows.bitcast(F32)
            for chunk in range(BANK // P):
                cols = slice(chunk * P, (chunk + 1) * P)
                nc.tensor.transpose(bank[:, cols], words[:, cols], ident[:])
            copy = nc.vector.tensor_copy if through_vector else nc.scalar.copy
            copy(
                out=grouped.bitcast(F32).rearrange("p (g r u) -> p g r u", g=PASSES, u=2),
                in_=bank[:].rearrange("p (g u r) -> p g r u", g=PASSES, u=2),
            )

        def mx_tiles(pool, tag, words):
            codes = pool.tile([P, words], U32, tag=tag + "_codes", align_bytes=64)
            scales = pool.tile([P, words], U8, tag=tag + "_scales", align_bytes=64)
            return codes, scales

        def operand(mx, first, words):
            codes, scales = mx
            return codes[:, first : first + words].bitcast(FP8X4), scales[:, first : first + words]

        def quantise(grouped, mx, first):
            codes, scales = operand(mx, first, grouped.shape[1] // PACK)
            nc.vector.quantize_mx(out=codes, scales=scales, in_=grouped)

        def first_matmul(x_q, j):
            v_ps = psum_v.tile([P, BANK], F32, tag="v_ps")
            for t in range(PACK):
                for g in range(PASSES):
                    x_codes, x_scales = operand(x_q, t * TILE_WORDS + g * P, P)
                    w_codes, w_scales = operand(w_q, j * TILE_WORDS + g * P, P)
                    nc.tensor.matmul_mx(
                        out=v_ps[:, t * P : (t + 1) * P],
                        lhsT=x_codes,
                        lhsT_scale=x_scales,
                        rhs=w_codes,
                        rhs_scale=w_scales,
                        start=(g == 0),
                        stop=(g == PASSES - 1),
                    )
            return v_ps

        def first_drain(v_ps, j, v_grouped):
            nc.vector.tensor_tensor(
                out=v_grouped[:, j * BANK : (j + 1) * BANK].rearrange("p (r t) -> p r t", t=PACK),
                in0=v_ps[:].rearrange("p (t r) -> p r t", t=PACK),
                in1=bias_by_tile[:, j, :].unsqueeze(2).to_broadcast([P, P, PACK]),
                op=ADD,
            )

        def second_matmul(b, v_q, att_q, j, out_sb, through_scalar):
            v_codes, v_scales = operand(v_q, j * P, P)
            att_codes, att_scales = operand(att_q, 0, L)
            o_ps = psum_s.tile([P, BANK], F32, tag="bank")
            nc.tensor.matmul_mx(
                out=o_ps[:],
                lhsT=v_codes,
                lhsT_scale=v_scales,
                rhs=att_codes,
                rhs_scale=att_scales,
                start=True,
                stop=True,
            )
            cols = slice(j * L, (j + 1) * L)
            if through_scalar:
                nc.scalar.activation(out=out_sb[:, cols], in_=o_ps[:], func=COPY, scale=gamma[:, 0:1])
                nc.gpsimd.tensor_tensor(
                    out=out_sb[:, cols], in0=out_sb[:, cols], in1=y_sb[b][:, cols], op=ADD
                )
            else:
                nc.vector.scalar_tensor_tensor(
                    out=out_sb[:, cols],
                    in0=o_ps[:],
                    scalar=gamma[:, 0:1],
                    in1=y_sb[b][:, cols],
                    op0=MULT,
                    op1=ADD,
                )

        def transpose_x(b, vector_tiles=()):
            x_grouped = stage.tile([P, PACK * D], BF16, tag="x_grouped", align_bytes=64)
            for t in range(PACK):
                cols = slice(t * D, (t + 1) * D)
                transpose_tile(x_sb[b][:, cols], x_grouped[:, cols], t in vector_tiles)
            return x_grouped

        def transpose_w(run, vector_tiles=()):
            w_grouped = stage.tile(
                [P, RUN * D], BF16, tag="w_grouped", bufs=W_AHEAD + 1, align_bytes=64
            )
            for i in range(RUN):
                j = run * RUN + i
                transpose_tile(w_sb[:, j * D : (j + 1) * D], w_grouped[:, i * D : (i + 1) * D], j in vector_tiles)
            return w_grouped

        def regroup_att(b):
            att_grouped = stage.tile([P, PACK * L], BF16, tag="att_grouped", align_bytes=64)
            nc.scalar.copy(
                out=att_grouped[:].rearrange("p (c i t) -> p c t i", i=4, t=PACK),
                in_=att_sb[b][:].rearrange("p (t c i) -> p c t i", t=PACK, i=4),
            )
            return att_grouped

        for i in range(WARM):
            idle = psum_v.tile([P, BANK], F32, tag="v_ps")
            nc.tensor.matmul(idle[:, :P], lhsT=ones[:], rhs=ones[:], start=True, stop=True)
        x_grouped = transpose_x(0, vector_tiles=())
        x_q = mx_tiles(stage, "x", PACK * TILE_WORDS)
        for t in range(PACK):
            quantise(x_grouped[:, t * D : (t + 1) * D], x_q, t * TILE_WORDS)
        w_q = mx_tiles(const, "w", D_TILES * TILE_WORDS)
        bias_by_tile = const.tile([P, D_TILES, P], F32)
        for half in range(D // BANK):
            bias_ps = psum_v.tile([P, BANK], F32, tag="v_ps")
            nc.tensor.matmul(
                bias_ps[:],
                lhsT=ones[:],
                rhs=bias_row[:, half * BANK : (half + 1) * BANK],
                start=True,
                stop=True,
            )
            rows = BANK // D_TILES
            nc.vector.tensor_copy(
                out=bias_by_tile[:, :, half * rows : (half + 1) * rows],
                in_=bias_ps[:].rearrange("p (r j) -> p j r", j=D_TILES),
            )
        w_grouped = [transpose_w(0)]
        gamma = const.tile([P, 1], F32)

        def quantise_w(run):
            quantise(w_grouped[run][:], w_q, run * RUN * TILE_WORDS)

        HALF = D_TILES * BANK // 2
        v_grouped = {}
        v_ps = {}
        v_q = {}
        att_grouped = {}
        att_q = {}
        out_sb = {}
        x_grouped = {}
        x_mx = {0: x_q}

        def run_plan(plan):
            for word in plan.split():
                kind, b, arg = word[0], int(word[1]), word[2:]
                if kind == "g":
                    nc.vector.tensor_copy(out=gamma[:], in_=gamma_bf[:])
                elif kind == "w":
                    w_grouped.append(transpose_w(b, vector_tiles=()))
                elif kind == "W":
                    quantise_w(b)
                elif kind == "t":
                    x_grouped[b] = transpose_x(b)
                elif kind == "r":
                    att_grouped[b] = regroup_att(b)
                elif kind == "x":
                    x_mx[b] = mx_tiles(stage, "x", PACK * TILE_WORDS)
                    quantise(x_grouped[b][:], x_mx[b], 0)
                elif kind == "a":
                    att_q[b] = mx_tiles(stage, "att", L)
                    quantise(att_grouped[b][:], att_q[b], 0)
                elif kind == "q":
                    first, last = int(arg[0]), int(arg[1])
                    if first == 0:
                        v_q[b] = mx_tiles(stage, "v", D_TILES * P)
                    quantise(v_grouped[b][:, first * BANK : last * BANK], v_q[b], first * P)
                elif kind == "v":
                    if arg == "0":
                        v_tile = stage.tile([P, D_TILES * BANK], BF16, tag="v_grouped", align_bytes=64)
                        v_grouped[b] = v_tile
                    first_drain(first_matmul(x_mx[b], int(arg)), int(arg), v_grouped[b])
                elif kind == "m":
                    v_ps[b, int(arg)] = first_matmul(x_mx[b], int(arg))
                elif kind == "d":
                    if arg == "0":
                        v_tile = stage.tile([P, D_TILES * BANK], BF16, tag="v_grouped", align_bytes=64)
                        v_grouped[b] = v_tile
                    first_drain(v_ps[b, int(arg)], int(arg), v_grouped[b])
                elif kind in "zy":
                    for i in range(b):
                        pool, tag = (psum_s, "bank") if kind == "z" else (psum_v, "v_ps")
                        idle = pool.tile([P, BANK], F32, tag=tag)
                        nc.tensor.matmul(idle[:], lhsT=ones[:], rhs=bias_row[:, :BANK], start=True, stop=True)
                elif kind in "SD":
                    j = int(arg)
                    if j == 0:
                        out_tile = stage.tile([P, D_TILES * L], F32, tag="out_sb")
                        out_sb[b] = out_tile
                    second_matmul(b, v_q[b], att_q[b], j, out_sb[b], kind == "S")
                elif kind == "o":
                    cols = slice(int(arg[0]) * L, int(arg[1]) * L)
                    nc.sync.dma_start(out=out[b].rearrange("(p a) c -> p (a c)", a=PACK)[:, cols], in_=out_sb[b][:, cols])

        for plan in PLANS:
            run_plan(plan)
